import numpy as np
import ml_dtypes


def mxq(x, axis, fmt="e4m3"):
    dtype, down = {"e4m3": (ml_dtypes.float8_e4m3fn, 7), "e5m2": (ml_dtypes.float8_e5m2, 14)}[fmt]
    v = np.moveaxis(np.asarray(x, np.float32).astype(ml_dtypes.bfloat16).astype(np.float64), axis, -1)
    blocks = v.reshape(v.shape[:-1] + (-1, 32))
    amax = np.abs(blocks).max(-1, keepdims=True)
    byte = np.maximum(np.where(amax > 0, np.frexp(amax)[1] - 1 + 127, 0) - down, 1)
    scale = np.exp2(byte - 127.0)
    codes = (blocks / scale).astype(np.float32).astype(dtype).astype(np.float64)
    return np.moveaxis((codes * scale).reshape(v.shape), -1, axis)


WIDE = False


def mx_kscale(k):
    if not WIDE:
        return np.ones(k)
    levels = np.array([30, -30])
    if k % 512:
        return np.exp2(np.random.permutation(np.resize(levels, k // 32))).repeat(32)
    a = np.empty((k // 512, 16))
    for p in range(k // 512):
        a[p, :8] = np.random.permutation(np.resize(levels, 8))
        for g in range(8):
            far = levels[np.abs(levels - a[p, g]) >= 10]
            a[p, g + 8] = far[np.random.randint(len(far))]
    return np.exp2(a.ravel()).repeat(32)


BF16 = ml_dtypes.bfloat16


def bf(x):
    return np.asarray(x, np.float32).astype(BF16)


def f64(x):
    return np.asarray(x).astype(np.float64)


E2M1 = np.array([0.0, 0.5, 1.0, 1.5, 2.0, 3.0, 4.0, 6.0, -0.0, -0.5, -1.0, -1.5, -2.0, -3.0, -4.0, -6.0])


def pack_weight(w, fmt):
    k, n = w.shape
    w = f64(bf(w)).reshape(k // 32, 32, n)
    amax = np.abs(w).max(1)
    if fmt == "e4m3":
        byte = np.frexp(amax)[1] - 1 + 127 - 7
    else:
        mant, ex = np.frexp(amax / 6.0)
        byte = np.where(mant > 0.5, ex, ex - 1) + 127
    byte = np.clip(np.where(amax > 0, byte, 1), 1, 254)
    scaled = (w * np.exp2(127.0 - byte)[:, None, :]).reshape(k, n).astype(np.float32)
    by_word = np.ascontiguousarray(scaled.reshape(k // 512, 128, 4, n).transpose(0, 1, 3, 2))
    if fmt == "e4m3":
        words = by_word.astype(ml_dtypes.float8_e4m3fn).view(np.uint8)
    else:
        c = by_word.astype(ml_dtypes.float4_e2m1fn).view(np.uint8) & 0xF
        words = c[..., 0::2] | (c[..., 1::2] << 4)
    return np.ascontiguousarray(words), np.ascontiguousarray(byte.astype(np.uint8).reshape(k // 512, 16, n))


def unpack_weight(words, scales, fmt):
    g, p, n, _ = words.shape
    if fmt == "e4m3":
        vals = np.ascontiguousarray(words).view(ml_dtypes.float8_e4m3fn).astype(np.float64)
    else:
        nib = np.empty((g, p, n, 4), np.uint8)
        nib[..., 0::2] = words & 0xF
        nib[..., 1::2] = words >> 4
        vals = E2M1[nib]
    vals = vals * np.repeat(np.exp2(scales.astype(np.float64) - 127.0), 8, axis=1)[..., None]
    return vals.transpose(0, 1, 3, 2).reshape(g * 512, n)

def pack4(w):
    words, scales = pack_weight(w, "e2m1")
    return words.reshape(words.shape[0], 128, -1), scales


def unpack4(words, scales):
    return unpack_weight(words.reshape(words.shape[0], 128, -1, 2), scales, "e2m1")


B, IDIM, HDIM, ODIM, S, DEPTH, NACT, NTOP = 1024, 512, 1024, 512, 128, 32, 3, 2


def sigmoid(v):
    return 1.0 / (1.0 + np.exp(-v))


def setup_inputs():
    s, t = mx_kscale(IDIM), mx_kscale(HDIM)
    x = bf(np.random.standard_normal((B, IDIM)) * s)
    hidden = bf(np.random.standard_normal((B, HDIM)) * t)
    stack_top = bf(np.random.standard_normal((B, NTOP, S)))
    Wi = np.random.standard_normal((HDIM, IDIM)) * 0.7 / np.sqrt(IDIM) / s
    bi = bf(np.random.standard_normal(HDIM) * 0.2)
    Wh = np.random.standard_normal((HDIM, HDIM)) * 0.7 / np.sqrt(HDIM) / t
    bh = bf(np.random.standard_normal(HDIM) * 0.2)
    W0 = bf(np.random.standard_normal((HDIM, S)) * 0.5 / np.sqrt(S))
    b0 = bf(np.random.standard_normal(HDIM) * 0.2)
    W1 = bf(np.random.standard_normal((HDIM, S)) * 0.5 / np.sqrt(S))
    b1 = bf(np.random.standard_normal(HDIM) * 0.2)
    Wi_words, Wi_scales = pack4(np.ascontiguousarray(Wi.T))
    Wh_words, Wh_scales = pack4(np.ascontiguousarray(Wh.T))
    return {"x": x,
            "hidden": hidden,
            "stack_top": stack_top,
            "Wi_words": Wi_words,
            "Wi_scales": Wi_scales,
            "bi": bi,
            "Wh_words": Wh_words,
            "Wh_scales": Wh_scales,
            "bh": bh,
            "W0": W0,
            "b0": b0,
            "W1": W1,
            "b1": b1}


def reference(x, hidden, stack_top, Wi_words, Wi_scales, bi, Wh_words, Wh_scales, bh, W0, b0, W1, b1):
    pre = ((mxq(f64(x), 1, "e5m2") @ unpack4(Wi_words, Wi_scales)) + f64(bi)
           + (mxq(f64(hidden), 1, "e5m2") @ unpack4(Wh_words, Wh_scales)) + f64(bh)
           + f64(stack_top)[:, 0] @ f64(W0).T + f64(b0)
           + f64(stack_top)[:, 1] @ f64(W1).T + f64(b1))
    return sigmoid(pre)

@@ -1,0 +1,243 @@
+from contextlib import ExitStack
+
+import concourse.mybir as mybir
+from concourse.masks import make_identity
+
+B, IDIM, HDIM, S = 1024, 512, 1024, 128
+FLOPS = 2 * B * HDIM * (IDIM + HDIM + 2 * S)
+
+F32 = mybir.dt.float32
+BF16 = mybir.dt.bfloat16
+I32 = mybir.dt.int32
+U32 = mybir.dt.uint32
+U8 = mybir.dt.uint8
+E5M2X4 = mybir.dt.float8_e5m2_x4
+E2M1X4 = mybir.dt.float4_e2m1fn_x4
+ADD = mybir.AluOpType.add
+SIGMOID = mybir.ActivationFunctionType.Sigmoid
+
+P = 128
+TILES = B // P
+HALF = 512
+PASSES = (IDIM + HDIM) // 512
+LOAD_GROUPS = [(0, 1), (1, 2), (2, 4), (4, 6), (6, 8)]
+
+
+def tile_stackrnn_pa_kernel(tc, x, hidden, stack_top, Wi_words, Wi_scales, bi, Wh_words, Wh_scales, bh,
+                                        W0, b0, W1, b1, out):
+    nc = tc.nc
+    with ExitStack() as ctx:
+        keep = ctx.enter_context(tc.tile_pool(name="keep", bufs=1))
+        work = ctx.enter_context(tc.tile_pool(name="work", bufs=3))
+        psum = ctx.enter_context(tc.psum_pool(name="psum", bufs=1))
+        ctx.enter_context(tc.manual_schedule())
+
+        x_rows = x.rearrange("(p i) k -> p i k", i=TILES)
+        h_rows = hidden.rearrange("(p i) k -> p i k", i=TILES)
+        st_rows = stack_top.rearrange("(p i) a s -> p i (a s)", i=TILES)
+        out_rows = out.rearrange("(p i) n -> p i n", i=TILES)
+
+        bank_xs = psum.tile([P, HALF], F32, name="bank_xs")
+        bank_h = psum.tile([P, HALF], F32, name="bank_h")
+        bank_mx = [psum.tile([P, HALF], F32, name="bank_mx%d" % c) for c in range(2)]
+        bank_plain = [[psum.tile([P, HALF], F32, name="bank_plain%d%d" % (a, c)) for c in range(2)] for a in range(2)]
+
+        x_sb, h_sb, st_sb = {}, {}, {}
+
+        def load_rows(rows, width, lo, hi, name, table):
+            t = keep.tile([P, hi - lo, width], BF16, name="%s%d" % (name, lo))
+            nc.sync.dma_start(out=t[:], in_=rows[:, lo:hi, :])
+            for i in range(lo, hi):
+                table[i] = t[:, i - lo, :]
+
+        def load_xh(group):
+            lo, hi = LOAD_GROUPS[group]
+            load_rows(x_rows, IDIM, lo, hi, "x", x_sb)
+            load_rows(h_rows, HDIM, lo, hi, "h", h_sb)
+
+        bias_rows = keep.tile([P, HDIM], BF16, name="bias_rows")
+        nc.vector.memset(bias_rows[:].bitcast(I32), 0)
+        ones = keep.tile([P, P], BF16, name="ones")
+        nc.vector.memset(ones[:], 1.0)
+
+        def load_bias(r):
+            nc.sync.dma_start(out=bias_rows[r:r + 1, :], in_=(bi, bh, b0, b1)[r].rearrange("(o n) -> o n", o=1))
+
+        load_rows(st_rows, 2 * S, 0, 2, "st", st_sb)
+        w_raw = {}
+        for c in range(2):
+            for a, w in enumerate((W0, W1)):
+                t = keep.tile([P, 4 * S], BF16, name="wraw%d%d" % (a, c))
+                nc.sync.dma_start(out=t[:], in_=w[HALF * c:HALF * (c + 1), :].rearrange("(p j) s -> p (j s)", j=4))
+                w_raw[(a, c)] = t
+        load_bias(0)
+        load_bias(1)
+        load_rows(x_rows, IDIM, 0, 1, "x", x_sb)
+        load_bias(2)
+        load_bias(3)
+        load_rows(h_rows, HDIM, 0, 1, "h", h_sb)
+        plane = keep.tile([P, PASSES, 4, HDIM], U8, name="plane", align_bytes=64)
+        nc.sync.dma_start(out=plane[0:4, 0, :, :].bitcast(I32),
+                          in_=Wi_scales[0].rearrange("(q r) n -> r q n", r=4).bitcast(I32))
+        nc.sync.dma_start(out=plane[0:4, 1:PASSES, :, :].rearrange("r g q n -> r (g q) n").bitcast(I32),
+                          in_=Wh_scales.rearrange("g (q r) n -> r (g q) n", r=4).bitcast(I32))
+        load_xh(1)
+        codes_w = {}
+        for c in range(2):
+            cols = slice(2 * HALF * c, 2 * HALF * (c + 1))
+            ti = keep.tile([P, 2 * HALF], U8, name="wi%d" % c, align_bytes=64)
+            nc.sync.dma_start(out=ti[:].bitcast(I32), in_=Wi_words[0][:, cols].bitcast(I32))
+            th = keep.tile([P, 2, 2 * HALF], U8, name="wh%d" % c, align_bytes=64)
+            nc.sync.dma_start(out=th[:].bitcast(I32),
+                              in_=Wh_words[:, :, cols].rearrange("g p n -> p g n").bitcast(I32))
+            codes_w[(0, c)] = ti[:]
+            codes_w[(1, c)] = th[:, 0, :]
+            codes_w[(2, c)] = th[:, 1, :]
+        load_rows(st_rows, 2 * S, 2, TILES, "st", st_sb)
+        for group in range(2, len(LOAD_GROUPS)):
+            load_xh(group)
+
+        ident_bf = keep.tile([P, P], BF16, name="ident_bf")
+        make_identity(nc, ident_bf[:])
+        ident_f32 = keep.tile([P, P], F32, name="ident_f32")
+        make_identity(nc, ident_f32[:])
+        bias = [keep.tile([P, HALF], F32, name="bias%d" % c) for c in range(2)]
+
+        st_t, x_grouped, h_grouped, codes, scales, plain, summed = {}, {}, {}, {}, {}, {}, {}
+        w_t = {}
+        st_bank = bank_xs[:, 2 * P:3 * P].bitcast(BF16)
+
+        def transpose_st(i, a):
+            nc.tensor.transpose(st_bank[:, P * a:P * (a + 1)], st_sb[i][:, S * a:S * (a + 1)], ident_bf[:])
+
+        def transpose_x(i, u):
+            words = x_sb[i].bitcast(F32)
+            nc.tensor.transpose(bank_xs[:, P * u:P * (u + 1)], words[:, u:2 * P:2], ident_f32[:])
+
+        def transpose_h(i, g, u):
+            words = h_sb[i].bitcast(F32)
+            nc.tensor.transpose(bank_h[:, P * (2 * g + u):P * (2 * g + u + 1)],
+                                words[:, 2 * P * g + u:2 * P * (g + 1):2], ident_f32[:])
+
+        def copy_st(i, engine_copy):
+            t = work.tile([P, 2 * P], BF16, name="st_t")
+            engine_copy(out=t[:], in_=st_bank)
+            st_t[i] = t
+
+        def copy_x(i):
+            t = work.tile([P, 4 * P], BF16, name="x_grouped", align_bytes=64)
+            nc.scalar.copy(out=t[:].bitcast(F32).rearrange("p (r u) -> p r u", u=2),
+                           in_=bank_xs[:, 0:2 * P].rearrange("p (u r) -> p r u", u=2))
+            x_grouped[i] = t
+
+        def copy_h(i):
+            t = work.tile([P, 8 * P], BF16, name="h_grouped", align_bytes=64)
+            nc.scalar.copy(out=t[:].bitcast(F32).rearrange("p (g r u) -> p g r u", g=2, u=2),
+                           in_=bank_h[:].rearrange("p (g u r) -> p g r u", g=2, u=2))
+            h_grouped[i] = t
+
+        def quantize_x(i):
+            q = work.tile([P, P], U32, name="x_codes", align_bytes=64)
+            s = work.tile([P, P], U8, name="x_scales", align_bytes=64)
+            nc.vector.quantize_mx(out=q[:].bitcast(E5M2X4), scales=s[:], in_=x_grouped[i][:])
+            codes[(i, 0)], scales[(i, 0)] = q[:], s[:]
+
+        def quantize_h(i):
+            q = work.tile([P, 2 * P], U32, name="h_codes", align_bytes=64)
+            s = work.tile([P, 2 * P], U8, name="h_scales", align_bytes=64)
+            nc.vector.quantize_mx(out=q[:].bitcast(E5M2X4), scales=s[:], in_=h_grouped[i][:])
+            for g in range(2):
+                codes[(i, 1 + g)], scales[(i, 1 + g)] = q[:, P * g:P * (g + 1)], s[:, P * g:P * (g + 1)]
+
+        def plain_products(i):
+            more = i + 1 < TILES
+            for c in range(2):
+                for a in range(2):
+                    nc.tensor.matmul(bank_plain[i % 2][c][:], lhsT=st_t[i][:, P * a:P * (a + 1)], rhs=w_t[(a, c)][:],
+                                     start=(a == 0), stop=(a == 1))
+                    if c == 0:
+                        if more:
+                            transpose_st(i + 1, a)
+                        transpose_x(i, a)
+                    else:
+                        transpose_h(i, a, 0)
+                        transpose_h(i, a, 1)
+
+        def add_bias(i, c):
+            t = work.tile([P, HALF], F32, name="plain", bufs=5)
+            nc.vector.tensor_tensor(out=t[:], in0=bank_plain[i % 2][c][:], in1=bias[c][:], op=ADD)
+            plain[(i, c)] = t
+
+        def mx_products(i, col, width, bank):
+            c, lo = divmod(col, HALF)
+            for g in range(PASSES):
+                nc.tensor.matmul_mx(out=bank[:, 0:width], lhsT=codes[(i, g)].bitcast(E5M2X4), lhsT_scale=scales[(i, g)],
+                                    rhs=codes_w[(g, c)][:, 2 * lo:2 * (lo + width)].bitcast(E2M1X4),
+                                    rhs_scale=plane[:, g, 0, col:col + width],
+                                    start=(g == 0), stop=(g == PASSES - 1))
+
+        def add_mx(i, col, width, bank):
+            c, lo = divmod(col, HALF)
+            t = work.tile([P, width], F32, name="summed", bufs=4)
+            nc.vector.tensor_tensor(out=t[:], in0=bank[:, 0:width], in1=plain[(i, c)][:, lo:lo + width], op=ADD)
+            summed[(i, col)] = t
+
+        def finish(i, col, width):
+            t = work.tile([P, width], F32, name="result", bufs=8)
+            nc.scalar.activation(out=t[:], in_=summed[(i, col)][:], func=SIGMOID)
+            nc.sync.dma_start(out=out_rows[:, i, col:col + width], in_=t[:])
+
+        transpose_st(0, 0)
+        transpose_st(0, 1)
+        copy_st(0, nc.vector.tensor_copy)
+        for c in range(2):
+            for a in range(2):
+                bank = (bank_mx, bank_plain[1])[c][a][:, 0:2 * P].bitcast(BF16)
+                for j in range(4):
+                    nc.tensor.transpose(bank[:, P * j:P * (j + 1)], w_raw[(a, c)][:, S * j:S * (j + 1)], ident_bf[:])
+                t = keep.tile([P, HALF], BF16, name="w_t%d%d" % (a, c))
+                (nc.scalar.copy, nc.vector.tensor_copy)[a](
+                    out=t[:].rearrange("k (p j) -> k p j", j=4), in_=bank.rearrange("k (j p) -> k p j", j=4))
+                w_t[(a, c)] = t
+
+        plain_products(0)
+        copy_x(0)
+        copy_st(1, nc.scalar.copy)
+        copy_h(0)
+        for g in range(PASSES):
+            for q in range(1, 4):
+                nc.vector.tensor_copy(out=plane[32 * q:32 * q + 4, g, 0, :].bitcast(I32),
+                                      in_=plane[0:4, g, q, :].bitcast(I32))
+        quantize_x(0)
+        quantize_h(0)
+        for c in range(2):
+            nc.tensor.matmul(bank_mx[c][:], lhsT=ones[:], rhs=bias_rows[:, HALF * c:HALF * (c + 1)], start=True, stop=True)
+            nc.scalar.copy(out=bias[c][:], in_=bank_mx[c][:])
+        add_bias(0, 0)
+        add_bias(0, 1)
+
+        for i in range(TILES - 1):
+            plain_products(i + 1)
+            copy_x(i + 1)
+            if i + 2 < TILES:
+                copy_st(i + 2, nc.scalar.copy)
+            if i > 0:
+                finish(i - 1, HALF, HALF)
+            copy_h(i + 1)
+            add_bias(i + 1, 0)
+            add_bias(i + 1, 1)
+            quantize_x(i + 1)
+            mx_products(i, 0, HALF, bank_mx[0])
+            add_mx(i, 0, HALF, bank_mx[0])
+            quantize_h(i + 1)
+            finish(i, 0, HALF)
+            mx_products(i, HALF, HALF, bank_mx[1])
+            add_mx(i, HALF, HALF, bank_mx[1])
+
+        last = TILES - 1
+        finish(last - 1, HALF, HALF)
+        pieces = [(0, HALF, bank_plain[0][0]), (HALF, HALF // 2, bank_plain[0][1]), (HALF + HALF // 2, HALF // 2, bank_h)]
+        for col, width, bank in pieces:
+            mx_products(last, col, width, bank)
+            add_mx(last, col, width, bank)
+            finish(last, col, width)

@@ -20,7 +20,7 @@ P = 128
 TILES = B // P
 HALF = 512
 PASSES = (IDIM + HDIM) // 512
-LOAD_GROUPS = [(0, 1), (1, 2), (2, 4), (4, 6), (6, 8)]
+LATER_GROUPS = [(2, 4), (4, 6), (6, 8)]
 
 
 def tile_stackrnn_pa_kernel(tc, x, hidden, stack_top, Wi_words, Wi_scales, bi, Wh_words, Wh_scales, bh,
@@ -50,52 +50,68 @@ def tile_stackrnn_pa_kernel(tc, x, hidden, stack_top, Wi_words, Wi_scales, bi, W
             for i in range(lo, hi):
                 table[i] = t[:, i - lo, :]
 
-        def load_xh(group):
-            lo, hi = LOAD_GROUPS[group]
-            load_rows(x_rows, IDIM, lo, hi, "x", x_sb)
-            load_rows(h_rows, HDIM, lo, hi, "h", h_sb)
-
         bias_rows = keep.tile([P, HDIM], BF16, name="bias_rows")
-        nc.vector.memset(bias_rows[:].bitcast(I32), 0)
+        nc.gpsimd.memset(bias_rows[:].bitcast(I32), 0)
         ones = keep.tile([P, P], BF16, name="ones")
         nc.vector.memset(ones[:], 1.0)
 
         def load_bias(r):
             nc.sync.dma_start(out=bias_rows[r:r + 1, :], in_=(bi, bh, b0, b1)[r].rearrange("(o n) -> o n", o=1))
 
-        load_rows(st_rows, 2 * S, 0, 2, "st", st_sb)
         w_raw = {}
-        for c in range(2):
-            for a, w in enumerate((W0, W1)):
-                t = keep.tile([P, 4 * S], BF16, name="wraw%d%d" % (a, c))
-                nc.sync.dma_start(out=t[:], in_=w[HALF * c:HALF * (c + 1), :].rearrange("(p j) s -> p (j s)", j=4))
-                w_raw[(a, c)] = t
+
+        def load_plain_weight(a):
+            t = keep.tile([P, 2, 4 * S], BF16, name="wraw%d" % a)
+            nc.sync.dma_start(out=t[:], in_=(W0, W1)[a].rearrange("(c p j) s -> p c (j s)", c=2, j=4))
+            w_raw[a] = t
+
+        codes_w = {}
+
+        def load_wi(c):
+            t = keep.tile([P, 2 * HALF], U8, name="wi%d" % c, align_bytes=64)
+            nc.sync.dma_start(out=t[:].bitcast(I32), in_=Wi_words[0][:, 2 * HALF * c:2 * HALF * (c + 1)].bitcast(I32))
+            codes_w[(0, c)] = t[:]
+
+        def load_wh(c):
+            t = keep.tile([P, 2, 2 * HALF], U8, name="wh%d" % c, align_bytes=64)
+            nc.sync.dma_start(out=t[:].bitcast(I32),
+                              in_=Wh_words[:, :, 2 * HALF * c:2 * HALF * (c + 1)].rearrange("g p n -> p g n").bitcast(I32))
+            codes_w[(1, c)] = t[:, 0, :]
+            codes_w[(2, c)] = t[:, 1, :]
+
+        plane_i = keep.tile([P, 1, HDIM], U8, name="plane_i", align_bytes=64)
+        plane_h = keep.tile([P, 2, HDIM], U8, name="plane_h", align_bytes=64)
+        planes = [plane_i[:, 0, :], plane_h[:, 0, :], plane_h[:, 1, :]]
+
+        def load_scales(plane, w_scales, r):
+            nc.sync.dma_start(out=plane[r:P:32, :, :].bitcast(I32),
+                              in_=w_scales[:, r:16:4, :].rearrange("g q n -> q g n").bitcast(I32))
+
+        load_rows(st_rows, 2 * S, 0, 3, "st", st_sb)
         load_bias(0)
         load_bias(1)
-        load_rows(x_rows, IDIM, 0, 1, "x", x_sb)
+        load_plain_weight(0)
         load_bias(2)
         load_bias(3)
-        load_rows(h_rows, HDIM, 0, 1, "h", h_sb)
-        plane = keep.tile([P, PASSES, 4, HDIM], U8, name="plane", align_bytes=64)
-        nc.sync.dma_start(out=plane[0:4, 0, :, :].bitcast(I32),
-                          in_=Wi_scales[0].rearrange("(q r) n -> r q n", r=4).bitcast(I32))
-        nc.sync.dma_start(out=plane[0:4, 1:PASSES, :, :].rearrange("r g q n -> r (g q) n").bitcast(I32),
-                          in_=Wh_scales.rearrange("g (q r) n -> r (g q) n", r=4).bitcast(I32))
-        load_xh(1)
-        codes_w = {}
-        for c in range(2):
-            cols = slice(2 * HALF * c, 2 * HALF * (c + 1))
-            ti = keep.tile([P, 2 * HALF], U8, name="wi%d" % c, align_bytes=64)
-            nc.sync.dma_start(out=ti[:].bitcast(I32), in_=Wi_words[0][:, cols].bitcast(I32))
-            th = keep.tile([P, 2, 2 * HALF], U8, name="wh%d" % c, align_bytes=64)
-            nc.sync.dma_start(out=th[:].bitcast(I32),
-                              in_=Wh_words[:, :, cols].rearrange("g p n -> p g n").bitcast(I32))
-            codes_w[(0, c)] = ti[:]
-            codes_w[(1, c)] = th[:, 0, :]
-            codes_w[(2, c)] = th[:, 1, :]
-        load_rows(st_rows, 2 * S, 2, TILES, "st", st_sb)
-        for group in range(2, len(LOAD_GROUPS)):
-            load_xh(group)
+        load_plain_weight(1)
+        load_rows(x_rows, IDIM, 0, 2, "x", x_sb)
+        for r in range(3):
+            load_scales(plane_i, Wi_scales, r)
+        load_rows(h_rows, HDIM, 0, 2, "h", h_sb)
+        load_scales(plane_i, Wi_scales, 3)
+        load_scales(plane_h, Wh_scales, 0)
+        load_scales(plane_h, Wh_scales, 1)
+        load_wi(0)
+        load_scales(plane_h, Wh_scales, 2)
+        load_scales(plane_h, Wh_scales, 3)
+        load_wh(0)
+        load_wi(1)
+        load_wh(1)
+        for lo, hi in LATER_GROUPS:
+            load_rows(x_rows, IDIM, lo, hi, "x", x_sb)
+            if lo == 2:
+                load_rows(st_rows, 2 * S, 3, TILES, "st", st_sb)
+            load_rows(h_rows, HDIM, lo, hi, "h", h_sb)
 
         ident_bf = keep.tile([P, P], BF16, name="ident_bf")
         make_identity(nc, ident_bf[:])
@@ -173,7 +189,7 @@ def tile_stackrnn_pa_kernel(tc, x, hidden, stack_top, Wi_words, Wi_scales, bi, W
             for g in range(PASSES):
                 nc.tensor.matmul_mx(out=bank[:, 0:width], lhsT=codes[(i, g)].bitcast(E5M2X4), lhsT_scale=scales[(i, g)],
                                     rhs=codes_w[(g, c)][:, 2 * lo:2 * (lo + width)].bitcast(E2M1X4),
-                                    rhs_scale=plane[:, g, 0, col:col + width],
+                                    rhs_scale=planes[g][:, col:col + width],
                                     start=(g == 0), stop=(g == PASSES - 1))
 
         def add_mx(i, col, width, bank):
@@ -190,31 +206,27 @@ def tile_stackrnn_pa_kernel(tc, x, hidden, stack_top, Wi_words, Wi_scales, bi, W
         transpose_st(0, 0)
         transpose_st(0, 1)
         copy_st(0, nc.vector.tensor_copy)
+        engine_copies = (nc.scalar.copy, nc.vector.tensor_copy)
         for c in range(2):
-            for a in range(2):
-                bank = (bank_mx, bank_plain[1])[c][a][:, 0:2 * P].bitcast(BF16)
+            nc.tensor.matmul(bank_plain[0][c][:], lhsT=ones[:], rhs=bias_rows[:, HALF * c:HALF * (c + 1)], start=True, stop=True)
+            engine_copies[c](out=bias[c][:], in_=bank_plain[0][c][:])
+        for a in range(2):
+            for c in range(2):
+                bank = (bank_mx, bank_plain[1])[a][c][:, 0:2 * P].bitcast(BF16)
                 for j in range(4):
-                    nc.tensor.transpose(bank[:, P * j:P * (j + 1)], w_raw[(a, c)][:, S * j:S * (j + 1)], ident_bf[:])
+                    nc.tensor.transpose(bank[:, P * j:P * (j + 1)], w_raw[a][:, c, S * j:S * (j + 1)], ident_bf[:])
                 t = keep.tile([P, HALF], BF16, name="w_t%d%d" % (a, c))
-                (nc.scalar.copy, nc.vector.tensor_copy)[a](
-                    out=t[:].rearrange("k (p j) -> k p j", j=4), in_=bank.rearrange("k (j p) -> k p j", j=4))
+                engine_copies[c](out=t[:].rearrange("k (p j) -> k p j", j=4), in_=bank.rearrange("k (j p) -> k p j", j=4))
                 w_t[(a, c)] = t
 
         plain_products(0)
         copy_x(0)
         copy_st(1, nc.scalar.copy)
         copy_h(0)
-        for g in range(PASSES):
-            for q in range(1, 4):
-                nc.vector.tensor_copy(out=plane[32 * q:32 * q + 4, g, 0, :].bitcast(I32),
-                                      in_=plane[0:4, g, q, :].bitcast(I32))
-        quantize_x(0)
-        quantize_h(0)
-        for c in range(2):
-            nc.tensor.matmul(bank_mx[c][:], lhsT=ones[:], rhs=bias_rows[:, HALF * c:HALF * (c + 1)], start=True, stop=True)
-            nc.scalar.copy(out=bias[c][:], in_=bank_mx[c][:])
         add_bias(0, 0)
         add_bias(0, 1)
+        quantize_x(0)
+        quantize_h(0)
 
         for i in range(TILES - 1):
             plain_products(i + 1)

@@ -109,9 +109,9 @@ def tile_stackrnn_pa_kernel(tc, x, hidden, stack_top, Wi_words, Wi_scales, bi, W
         load_wh(1)
         for lo, hi in LATER_GROUPS:
             load_rows(x_rows, IDIM, lo, hi, "x", x_sb)
+            load_rows(h_rows, HDIM, lo, hi, "h", h_sb)
             if lo == 2:
                 load_rows(st_rows, 2 * S, 3, TILES, "st", st_sb)
-            load_rows(h_rows, HDIM, lo, hi, "h", h_sb)
 
         ident_bf = keep.tile([P, P], BF16, name="ident_bf")
         make_identity(nc, ident_bf[:])
@@ -120,20 +120,25 @@ def tile_stackrnn_pa_kernel(tc, x, hidden, stack_top, Wi_words, Wi_scales, bi, W
         bias = [keep.tile([P, HALF], F32, name="bias%d" % c) for c in range(2)]
 
         st_t, x_grouped, h_grouped, codes, scales, plain, summed = {}, {}, {}, {}, {}, {}, {}
-        w_t = {}
+        w_t, x_split, h_split = {}, {}, {}
         st_bank = bank_xs[:, 2 * P:3 * P].bitcast(BF16)
 
         def transpose_st(i, a):
             nc.tensor.transpose(st_bank[:, P * a:P * (a + 1)], st_sb[i][:, S * a:S * (a + 1)], ident_bf[:])
 
+        def split(i, engine):
+            tx = work.tile([P, 2, P], F32, name="x_split", bufs=2)
+            engine.tensor_copy(out=tx[:].bitcast(I32), in_=x_sb[i].bitcast(I32).rearrange("b (p u) -> b u p", u=2))
+            th = work.tile([P, 2, 2, P], F32, name="h_split", bufs=2)
+            engine.tensor_copy(out=th[:].bitcast(I32),
+                               in_=h_sb[i].bitcast(I32).rearrange("b (g p u) -> b g u p", g=2, u=2))
+            x_split[i], h_split[i] = tx, th
+
         def transpose_x(i, u):
-            words = x_sb[i].bitcast(F32)
-            nc.tensor.transpose(bank_xs[:, P * u:P * (u + 1)], words[:, u:2 * P:2], ident_f32[:])
+            nc.tensor.transpose(bank_xs[:, P * u:P * (u + 1)], x_split[i][:, u, :], ident_f32[:])
 
         def transpose_h(i, g, u):
-            words = h_sb[i].bitcast(F32)
-            nc.tensor.transpose(bank_h[:, P * (2 * g + u):P * (2 * g + u + 1)],
-                                words[:, 2 * P * g + u:2 * P * (g + 1):2], ident_f32[:])
+            nc.tensor.transpose(bank_h[:, P * (2 * g + u):P * (2 * g + u + 1)], h_split[i][:, g, u, :], ident_f32[:])
 
         def copy_st(i, engine_copy):
             t = work.tile([P, 2 * P], BF16, name="st_t")
@@ -218,6 +223,8 @@ def tile_stackrnn_pa_kernel(tc, x, hidden, stack_top, Wi_words, Wi_scales, bi, W
                 t = keep.tile([P, HALF], BF16, name="w_t%d%d" % (a, c))
                 engine_copies[c](out=t[:].rearrange("k (p j) -> k p j", j=4), in_=bank.rearrange("k (j p) -> k p j", j=4))
                 w_t[(a, c)] = t
+        split(0, nc.vector)
+        split(1, nc.gpsimd)
 
         plain_products(0)
         copy_x(0)
@@ -229,6 +236,8 @@ def tile_stackrnn_pa_kernel(tc, x, hidden, stack_top, Wi_words, Wi_scales, bi, W
         quantize_h(0)
 
         for i in range(TILES - 1):
+            if i + 2 < TILES:
+                split(i + 2, nc.gpsimd)
             plain_products(i + 1)
             copy_x(i + 1)
             if i + 2 < TILES:

@@ -20,7 +20,9 @@ P = 128
 TILES = B // P
 HALF = 512
 PASSES = (IDIM + HDIM) // 512
-LATER_GROUPS = [(2, 4), (4, 6), (6, 8)]
+QUADRANT = 32
+ST_EARLY = 4
+VECTOR_SORTED = 2
 
 
 def tile_stackrnn_pa_kernel(tc, x, hidden, stack_top, Wi_words, Wi_scales, bi, Wh_words, Wh_scales, bh,
@@ -32,17 +34,18 @@ def tile_stackrnn_pa_kernel(tc, x, hidden, stack_top, Wi_words, Wi_scales, bi, W
         psum = ctx.enter_context(tc.psum_pool(name="psum", bufs=1))
         ctx.enter_context(tc.manual_schedule())
 
-        x_rows = x.rearrange("(p i) k -> p i k", i=TILES)
-        h_rows = hidden.rearrange("(p i) k -> p i k", i=TILES)
-        st_rows = stack_top.rearrange("(p i) a s -> p i (a s)", i=TILES)
-        out_rows = out.rearrange("(p i) n -> p i n", i=TILES)
+        x_rows = x.rearrange("(b i) k -> b i k", i=TILES)
+        h_rows = hidden.rearrange("(b i) k -> b i k", i=TILES)
+        st_rows = stack_top.rearrange("(b i) a s -> b i (a s)", i=TILES)
+        out_rows = out.rearrange("(b i) n -> b i n", i=TILES)
 
         bank_xs = psum.tile([P, HALF], F32, name="bank_xs")
         bank_h = psum.tile([P, HALF], F32, name="bank_h")
         bank_mx = [psum.tile([P, HALF], F32, name="bank_mx%d" % c) for c in range(2)]
-        bank_plain = [[psum.tile([P, HALF], F32, name="bank_plain%d%d" % (a, c)) for c in range(2)] for a in range(2)]
+        bank_plain = [[psum.tile([P, HALF], F32, name="bank_plain%d%d" % (odd, c)) for c in range(2)]
+                      for odd in range(2)]
 
-        x_sb, h_sb, st_sb = {}, {}, {}
+        x_sb, h_sb, st_sb, w_raw, w_codes = {}, {}, {}, {}, {}
 
         def load_rows(rows, width, lo, hi, name, table):
             t = keep.tile([P, hi - lo, width], BF16, name="%s%d" % (name, lo))
@@ -50,68 +53,73 @@ def tile_stackrnn_pa_kernel(tc, x, hidden, stack_top, Wi_words, Wi_scales, bi, W
             for i in range(lo, hi):
                 table[i] = t[:, i - lo, :]
 
+        def load_x(lo, hi):
+            load_rows(x_rows, IDIM, lo, hi, "x", x_sb)
+
+        def load_h(lo, hi):
+            load_rows(h_rows, HDIM, lo, hi, "h", h_sb)
+
+        def load_st(lo, hi):
+            load_rows(st_rows, 2 * S, lo, hi, "st", st_sb)
+
         bias_rows = keep.tile([P, HDIM], BF16, name="bias_rows")
         nc.gpsimd.memset(bias_rows[:].bitcast(I32), 0)
         ones = keep.tile([P, P], BF16, name="ones")
         nc.vector.memset(ones[:], 1.0)
 
-        def load_bias(r):
-            nc.sync.dma_start(out=bias_rows[r:r + 1, :], in_=(bi, bh, b0, b1)[r].rearrange("(o n) -> o n", o=1))
-
-        w_raw = {}
+        def load_bias(row):
+            nc.sync.dma_start(out=bias_rows[row:row + 1, :], in_=(bi, bh, b0, b1)[row].rearrange("(o n) -> o n", o=1))
 
         def load_plain_weight(a):
-            t = keep.tile([P, 2, 4 * S], BF16, name="wraw%d" % a)
+            t = keep.tile([P, 2, 4 * S], BF16, name="w_raw%d" % a)
             nc.sync.dma_start(out=t[:], in_=(W0, W1)[a].rearrange("(c p j) s -> p c (j s)", c=2, j=4))
             w_raw[a] = t
-
-        codes_w = {}
 
         def load_wi(c):
             t = keep.tile([P, 2 * HALF], U8, name="wi%d" % c, align_bytes=64)
             nc.sync.dma_start(out=t[:].bitcast(I32), in_=Wi_words[0][:, 2 * HALF * c:2 * HALF * (c + 1)].bitcast(I32))
-            codes_w[(0, c)] = t[:]
+            w_codes[(0, c)] = t[:]
 
         def load_wh(c):
             t = keep.tile([P, 2, 2 * HALF], U8, name="wh%d" % c, align_bytes=64)
             nc.sync.dma_start(out=t[:].bitcast(I32),
                               in_=Wh_words[:, :, 2 * HALF * c:2 * HALF * (c + 1)].rearrange("g p n -> p g n").bitcast(I32))
-            codes_w[(1, c)] = t[:, 0, :]
-            codes_w[(2, c)] = t[:, 1, :]
+            w_codes[(1, c)] = t[:, 0, :]
+            w_codes[(2, c)] = t[:, 1, :]
 
-        plane_i = keep.tile([P, 1, HDIM], U8, name="plane_i", align_bytes=64)
-        plane_h = keep.tile([P, 2, HDIM], U8, name="plane_h", align_bytes=64)
-        planes = [plane_i[:, 0, :], plane_h[:, 0, :], plane_h[:, 1, :]]
+        wi_scales = keep.tile([P, 1, HDIM], U8, name="wi_scales", align_bytes=64)
+        wh_scales = keep.tile([P, 2, HDIM], U8, name="wh_scales", align_bytes=64)
+        w_scales = [wi_scales[:, 0, :], wh_scales[:, 0, :], wh_scales[:, 1, :]]
 
-        def load_scales(plane, w_scales, r):
-            nc.sync.dma_start(out=plane[r:P:32, :, :].bitcast(I32),
-                              in_=w_scales[:, r:16:4, :].rearrange("g q n -> q g n").bitcast(I32))
+        def load_scale_rows(tile, source, r):
+            nc.sync.dma_start(out=tile[r:P:QUADRANT, :, :].bitcast(I32),
+                              in_=source[:, r:16:4, :].rearrange("g q n -> q g n").bitcast(I32))
 
-        load_rows(st_rows, 2 * S, 0, 3, "st", st_sb)
-        load_bias(0)
-        load_bias(1)
-        load_plain_weight(0)
-        load_bias(2)
-        load_bias(3)
-        load_plain_weight(1)
-        load_rows(x_rows, IDIM, 0, 2, "x", x_sb)
-        for r in range(3):
-            load_scales(plane_i, Wi_scales, r)
-        load_rows(h_rows, HDIM, 0, 2, "h", h_sb)
-        load_scales(plane_i, Wi_scales, 3)
-        load_scales(plane_h, Wh_scales, 0)
-        load_scales(plane_h, Wh_scales, 1)
+        load_st(0, ST_EARLY)
+        for a in range(2):
+            load_bias(2 * a)
+            load_bias(2 * a + 1)
+            load_plain_weight(a)
+        load_x(0, 2)
+        load_h(0, 1)
+        load_h(1, 2)
+        load_scale_rows(wi_scales, Wi_scales, 0)
+        load_scale_rows(wi_scales, Wi_scales, 1)
         load_wi(0)
-        load_scales(plane_h, Wh_scales, 2)
-        load_scales(plane_h, Wh_scales, 3)
+        load_scale_rows(wi_scales, Wi_scales, 2)
+        load_scale_rows(wi_scales, Wi_scales, 3)
         load_wh(0)
+        for r in range(4):
+            load_scale_rows(wh_scales, Wh_scales, r)
         load_wi(1)
         load_wh(1)
-        for lo, hi in LATER_GROUPS:
-            load_rows(x_rows, IDIM, lo, hi, "x", x_sb)
-            load_rows(h_rows, HDIM, lo, hi, "h", h_sb)
-            if lo == 2:
-                load_rows(st_rows, 2 * S, 3, TILES, "st", st_sb)
+        for i in range(2, ST_EARLY):
+            load_x(i, i + 1)
+            load_h(i, i + 1)
+        load_st(ST_EARLY, TILES)
+        for i in range(ST_EARLY, TILES, 2):
+            load_x(i, i + 2)
+            load_h(i, i + 2)
 
         ident_bf = keep.tile([P, P], BF16, name="ident_bf")
         make_identity(nc, ident_bf[:])
@@ -119,26 +127,27 @@ def tile_stackrnn_pa_kernel(tc, x, hidden, stack_top, Wi_words, Wi_scales, bi, W
         make_identity(nc, ident_f32[:])
         bias = [keep.tile([P, HALF], F32, name="bias%d" % c) for c in range(2)]
 
-        st_t, x_grouped, h_grouped, codes, scales, plain, summed = {}, {}, {}, {}, {}, {}, {}
-        w_t, x_split, h_split = {}, {}, {}
+        x_sorted, h_sorted, x_grouped, h_grouped, st_t, w_t = {}, {}, {}, {}, {}, {}
+        codes, scales, plain, summed = {}, {}, {}, {}
         st_bank = bank_xs[:, 2 * P:3 * P].bitcast(BF16)
+
+        def sort_words(i):
+            engine = nc.vector if i < VECTOR_SORTED else nc.gpsimd
+            tx = work.tile([P, 2, P], F32, name="x_sorted", bufs=2)
+            engine.tensor_copy(out=tx[:].bitcast(I32), in_=x_sb[i].bitcast(I32).rearrange("b (p u) -> b u p", u=2))
+            th = work.tile([P, 2, 2, P], F32, name="h_sorted", bufs=2)
+            engine.tensor_copy(out=th[:].bitcast(I32),
+                               in_=h_sb[i].bitcast(I32).rearrange("b (g p u) -> b g u p", g=2, u=2))
+            x_sorted[i], h_sorted[i] = tx, th
 
         def transpose_st(i, a):
             nc.tensor.transpose(st_bank[:, P * a:P * (a + 1)], st_sb[i][:, S * a:S * (a + 1)], ident_bf[:])
 
-        def split(i, engine):
-            tx = work.tile([P, 2, P], F32, name="x_split", bufs=2)
-            engine.tensor_copy(out=tx[:].bitcast(I32), in_=x_sb[i].bitcast(I32).rearrange("b (p u) -> b u p", u=2))
-            th = work.tile([P, 2, 2, P], F32, name="h_split", bufs=2)
-            engine.tensor_copy(out=th[:].bitcast(I32),
-                               in_=h_sb[i].bitcast(I32).rearrange("b (g p u) -> b g u p", g=2, u=2))
-            x_split[i], h_split[i] = tx, th
-
         def transpose_x(i, u):
-            nc.tensor.transpose(bank_xs[:, P * u:P * (u + 1)], x_split[i][:, u, :], ident_f32[:])
+            nc.tensor.transpose(bank_xs[:, P * u:P * (u + 1)], x_sorted[i][:, u, :], ident_f32[:])
 
         def transpose_h(i, g, u):
-            nc.tensor.transpose(bank_h[:, P * (2 * g + u):P * (2 * g + u + 1)], h_split[i][:, g, u, :], ident_f32[:])
+            nc.tensor.transpose(bank_h[:, P * (2 * g + u):P * (2 * g + u + 1)], h_sorted[i][:, g, u, :], ident_f32[:])
 
         def copy_st(i, engine_copy):
             t = work.tile([P, 2 * P], BF16, name="st_t")
@@ -147,14 +156,14 @@ def tile_stackrnn_pa_kernel(tc, x, hidden, stack_top, Wi_words, Wi_scales, bi, W
 
         def copy_x(i):
             t = work.tile([P, 4 * P], BF16, name="x_grouped", align_bytes=64)
-            nc.scalar.copy(out=t[:].bitcast(F32).rearrange("p (r u) -> p r u", u=2),
-                           in_=bank_xs[:, 0:2 * P].rearrange("p (u r) -> p r u", u=2))
+            nc.scalar.copy(out=t[:].bitcast(F32).rearrange("p (b u) -> p b u", u=2),
+                           in_=bank_xs[:, 0:2 * P].rearrange("p (u b) -> p b u", u=2))
             x_grouped[i] = t
 
         def copy_h(i):
             t = work.tile([P, 8 * P], BF16, name="h_grouped", align_bytes=64)
-            nc.scalar.copy(out=t[:].bitcast(F32).rearrange("p (g r u) -> p g r u", g=2, u=2),
-                           in_=bank_h[:].rearrange("p (g u r) -> p g r u", g=2, u=2))
+            nc.scalar.copy(out=t[:].bitcast(F32).rearrange("p (g b u) -> p g b u", g=2, u=2),
+                           in_=bank_h[:].rearrange("p (g u b) -> p g b u", g=2, u=2))
             h_grouped[i] = t
 
         def quantize_x(i):
@@ -170,14 +179,13 @@ def tile_stackrnn_pa_kernel(tc, x, hidden, stack_top, Wi_words, Wi_scales, bi, W
             for g in range(2):
                 codes[(i, 1 + g)], scales[(i, 1 + g)] = q[:, P * g:P * (g + 1)], s[:, P * g:P * (g + 1)]
 
-        def plain_products(i):
-            more = i + 1 < TILES
+        def plain_products_and_transposes(i):
             for c in range(2):
                 for a in range(2):
                     nc.tensor.matmul(bank_plain[i % 2][c][:], lhsT=st_t[i][:, P * a:P * (a + 1)], rhs=w_t[(a, c)][:],
                                      start=(a == 0), stop=(a == 1))
                     if c == 0:
-                        if more:
+                        if i + 1 < TILES:
                             transpose_st(i + 1, a)
                         transpose_x(i, a)
                     else:
@@ -193,8 +201,8 @@ def tile_stackrnn_pa_kernel(tc, x, hidden, stack_top, Wi_words, Wi_scales, bi, W
             c, lo = divmod(col, HALF)
             for g in range(PASSES):
                 nc.tensor.matmul_mx(out=bank[:, 0:width], lhsT=codes[(i, g)].bitcast(E5M2X4), lhsT_scale=scales[(i, g)],
-                                    rhs=codes_w[(g, c)][:, 2 * lo:2 * (lo + width)].bitcast(E2M1X4),
-                                    rhs_scale=planes[g][:, col:col + width],
+                                    rhs=w_codes[(g, c)][:, 2 * lo:2 * (lo + width)].bitcast(E2M1X4),
+                                    rhs_scale=w_scales[g][:, col:col + width],
                                     start=(g == 0), stop=(g == PASSES - 1))
 
         def add_mx(i, col, width, bank):
@@ -211,22 +219,24 @@ def tile_stackrnn_pa_kernel(tc, x, hidden, stack_top, Wi_words, Wi_scales, bi, W
         transpose_st(0, 0)
         transpose_st(0, 1)
         copy_st(0, nc.vector.tensor_copy)
-        engine_copies = (nc.scalar.copy, nc.vector.tensor_copy)
+        copy_of_half = (nc.scalar.copy, nc.vector.tensor_copy)
         for c in range(2):
-            nc.tensor.matmul(bank_plain[0][c][:], lhsT=ones[:], rhs=bias_rows[:, HALF * c:HALF * (c + 1)], start=True, stop=True)
-            engine_copies[c](out=bias[c][:], in_=bank_plain[0][c][:])
+            nc.tensor.matmul(bank_plain[0][c][:], lhsT=ones[:], rhs=bias_rows[:, HALF * c:HALF * (c + 1)],
+                             start=True, stop=True)
+            copy_of_half[c](out=bias[c][:], in_=bank_plain[0][c][:])
         for a in range(2):
             for c in range(2):
                 bank = (bank_mx, bank_plain[1])[a][c][:, 0:2 * P].bitcast(BF16)
                 for j in range(4):
                     nc.tensor.transpose(bank[:, P * j:P * (j + 1)], w_raw[a][:, c, S * j:S * (j + 1)], ident_bf[:])
                 t = keep.tile([P, HALF], BF16, name="w_t%d%d" % (a, c))
-                engine_copies[c](out=t[:].rearrange("k (p j) -> k p j", j=4), in_=bank.rearrange("k (j p) -> k p j", j=4))
+                copy_of_half[c](out=t[:].rearrange("k (p j) -> k p j", j=4),
+                                in_=bank.rearrange("k (j p) -> k p j", j=4))
                 w_t[(a, c)] = t
-        split(0, nc.vector)
-        split(1, nc.gpsimd)
+        sort_words(0)
+        sort_words(1)
 
-        plain_products(0)
+        plain_products_and_transposes(0)
         copy_x(0)
         copy_st(1, nc.scalar.copy)
         copy_h(0)
@@ -235,10 +245,11 @@ def tile_stackrnn_pa_kernel(tc, x, hidden, stack_top, Wi_words, Wi_scales, bi, W
         quantize_x(0)
         quantize_h(0)
 
-        for i in range(TILES - 1):
+        last = TILES - 1
+        for i in range(last):
             if i + 2 < TILES:
-                split(i + 2, nc.gpsimd)
-            plain_products(i + 1)
+                sort_words(i + 2)
+            plain_products_and_transposes(i + 1)
             copy_x(i + 1)
             if i + 2 < TILES:
                 copy_st(i + 2, nc.scalar.copy)
@@ -248,16 +259,19 @@ def tile_stackrnn_pa_kernel(tc, x, hidden, stack_top, Wi_words, Wi_scales, bi, W
             add_bias(i + 1, 0)
             add_bias(i + 1, 1)
             quantize_x(i + 1)
+            if i + 1 == last:
+                quantize_h(last)
             mx_products(i, 0, HALF, bank_mx[0])
             add_mx(i, 0, HALF, bank_mx[0])
-            quantize_h(i + 1)
+            if i + 1 < last:
+                quantize_h(i + 1)
             finish(i, 0, HALF)
             mx_products(i, HALF, HALF, bank_mx[1])
             add_mx(i, HALF, HALF, bank_mx[1])
 
-        last = TILES - 1
         finish(last - 1, HALF, HALF)
-        pieces = [(0, HALF, bank_plain[0][0]), (HALF, HALF // 2, bank_plain[0][1]), (HALF + HALF // 2, HALF // 2, bank_h)]
+        quarter = HALF // 2
+        pieces = [(0, HALF, bank_plain[0][0]), (HALF, quarter, bank_plain[0][1]), (HALF + quarter, quarter, bank_h)]
         for col, width, bank in pieces:
             mx_products(last, col, width, bank)
             add_mx(last, col, width, bank)

from contextlib import ExitStack

import concourse.mybir as mybir
from concourse.masks import make_identity

B, IDIM, HDIM, S = 1024, 512, 1024, 128
FLOPS = 2 * B * HDIM * (IDIM + HDIM + 2 * S)

F32 = mybir.dt.float32
BF16 = mybir.dt.bfloat16
I32 = mybir.dt.int32
U32 = mybir.dt.uint32
U8 = mybir.dt.uint8
E5M2X4 = mybir.dt.float8_e5m2_x4
E2M1X4 = mybir.dt.float4_e2m1fn_x4
ADD = mybir.AluOpType.add
SIGMOID = mybir.ActivationFunctionType.Sigmoid

P = 128
TILES = B // P
HALF = 512
PASSES = (IDIM + HDIM) // 512
QUADRANT = 32
ST_EARLY = 4
VECTOR_SORTED = 2


def tile_stackrnn_pa_kernel(tc, x, hidden, stack_top, Wi_words, Wi_scales, bi, Wh_words, Wh_scales, bh,
                                        W0, b0, W1, b1, out):
    nc = tc.nc
    with ExitStack() as ctx:
        keep = ctx.enter_context(tc.tile_pool(name="keep", bufs=1))
        work = ctx.enter_context(tc.tile_pool(name="work", bufs=3))
        psum = ctx.enter_context(tc.psum_pool(name="psum", bufs=1))
        ctx.enter_context(tc.manual_schedule())

        x_rows = x.rearrange("(b i) k -> b i k", i=TILES)
        h_rows = hidden.rearrange("(b i) k -> b i k", i=TILES)
        st_rows = stack_top.rearrange("(b i) a s -> b i (a s)", i=TILES)
        out_rows = out.rearrange("(b i) n -> b i n", i=TILES)

        bank_xs = psum.tile([P, HALF], F32, name="bank_xs")
        bank_h = psum.tile([P, HALF], F32, name="bank_h")
        bank_mx = [psum.tile([P, HALF], F32, name="bank_mx%d" % c) for c in range(2)]
        bank_plain = [[psum.tile([P, HALF], F32, name="bank_plain%d%d" % (odd, c)) for c in range(2)]
                      for odd in range(2)]

        x_sb, h_sb, st_sb, w_raw, w_codes = {}, {}, {}, {}, {}

        def load_rows(rows, width, lo, hi, name, table):
            t = keep.tile([P, hi - lo, width], BF16, name="%s%d" % (name, lo))
            nc.sync.dma_start(out=t[:], in_=rows[:, lo:hi, :])
            for i in range(lo, hi):
                table[i] = t[:, i - lo, :]

        def load_x(lo, hi):
            load_rows(x_rows, IDIM, lo, hi, "x", x_sb)

        def load_h(lo, hi):
            load_rows(h_rows, HDIM, lo, hi, "h", h_sb)

        def load_st(lo, hi):
            load_rows(st_rows, 2 * S, lo, hi, "st", st_sb)

        bias_rows = keep.tile([P, HDIM], BF16, name="bias_rows")
        nc.gpsimd.memset(bias_rows[:].bitcast(I32), 0)
        ones = keep.tile([P, P], BF16, name="ones")
        nc.vector.memset(ones[:], 1.0)

        def load_bias(row):
            nc.sync.dma_start(out=bias_rows[row:row + 1, :], in_=(bi, bh, b0, b1)[row].rearrange("(o n) -> o n", o=1))

        def load_plain_weight(a):
            t = keep.tile([P, 2, 4 * S], BF16, name="w_raw%d" % a)
            nc.sync.dma_start(out=t[:], in_=(W0, W1)[a].rearrange("(c p j) s -> p c (j s)", c=2, j=4))
            w_raw[a] = t

        def load_wi(c):
            t = keep.tile([P, 2 * HALF], U8, name="wi%d" % c, align_bytes=64)
            nc.sync.dma_start(out=t[:].bitcast(I32), in_=Wi_words[0][:, 2 * HALF * c:2 * HALF * (c + 1)].bitcast(I32))
            w_codes[(0, c)] = t[:]

        def load_wh(c):
            t = keep.tile([P, 2, 2 * HALF], U8, name="wh%d" % c, align_bytes=64)
            nc.sync.dma_start(out=t[:].bitcast(I32),
                              in_=Wh_words[:, :, 2 * HALF * c:2 * HALF * (c + 1)].rearrange("g p n -> p g n").bitcast(I32))
            w_codes[(1, c)] = t[:, 0, :]
            w_codes[(2, c)] = t[:, 1, :]

        wi_scales = keep.tile([P, 1, HDIM], U8, name="wi_scales", align_bytes=64)
        wh_scales = keep.tile([P, 2, HDIM], U8, name="wh_scales", align_bytes=64)
        w_scales = [wi_scales[:, 0, :], wh_scales[:, 0, :], wh_scales[:, 1, :]]

        def load_scale_rows(tile, source, r):
            nc.sync.dma_start(out=tile[r:P:QUADRANT, :, :].bitcast(I32),
                              in_=source[:, r:16:4, :].rearrange("g q n -> q g n").bitcast(I32))

        load_st(0, ST_EARLY)
        for a in range(2):
            load_bias(2 * a)
            load_bias(2 * a + 1)
            load_plain_weight(a)
        load_x(0, 2)
        load_h(0, 1)
        load_h(1, 2)
        load_scale_rows(wi_scales, Wi_scales, 0)
        load_scale_rows(wi_scales, Wi_scales, 1)
        load_wi(0)
        load_scale_rows(wi_scales, Wi_scales, 2)
        load_scale_rows(wi_scales, Wi_scales, 3)
        load_wh(0)
        for r in range(4):
            load_scale_rows(wh_scales, Wh_scales, r)
        load_wi(1)
        load_wh(1)
        for i in range(2, ST_EARLY):
            load_x(i, i + 1)
            load_h(i, i + 1)
        load_st(ST_EARLY, TILES)
        for i in range(ST_EARLY, TILES, 2):
            load_x(i, i + 2)
            load_h(i, i + 2)

        ident_bf = keep.tile([P, P], BF16, name="ident_bf")
        make_identity(nc, ident_bf[:])
        ident_f32 = keep.tile([P, P], F32, name="ident_f32")
        make_identity(nc, ident_f32[:])
        bias = [keep.tile([P, HALF], F32, name="bias%d" % c) for c in range(2)]

        x_sorted, h_sorted, x_grouped, h_grouped, st_t, w_t = {}, {}, {}, {}, {}, {}
        codes, scales, plain, summed = {}, {}, {}, {}
        st_bank = bank_xs[:, 2 * P:3 * P].bitcast(BF16)

        def sort_words(i):
            engine = nc.vector if i < VECTOR_SORTED else nc.gpsimd
            tx = work.tile([P, 2, P], F32, name="x_sorted", bufs=2)
            engine.tensor_copy(out=tx[:].bitcast(I32), in_=x_sb[i].bitcast(I32).rearrange("b (p u) -> b u p", u=2))
            th = work.tile([P, 2, 2, P], F32, name="h_sorted", bufs=2)
            engine.tensor_copy(out=th[:].bitcast(I32),
                               in_=h_sb[i].bitcast(I32).rearrange("b (g p u) -> b g u p", g=2, u=2))
            x_sorted[i], h_sorted[i] = tx, th

        def transpose_st(i, a):
            nc.tensor.transpose(st_bank[:, P * a:P * (a + 1)], st_sb[i][:, S * a:S * (a + 1)], ident_bf[:])

        def transpose_x(i, u):
            nc.tensor.transpose(bank_xs[:, P * u:P * (u + 1)], x_sorted[i][:, u, :], ident_f32[:])

        def transpose_h(i, g, u):
            nc.tensor.transpose(bank_h[:, P * (2 * g + u):P * (2 * g + u + 1)], h_sorted[i][:, g, u, :], ident_f32[:])

        def copy_st(i, engine_copy):
            t = work.tile([P, 2 * P], BF16, name="st_t")
            engine_copy(out=t[:], in_=st_bank)
            st_t[i] = t

        def copy_x(i):
            t = work.tile([P, 4 * P], BF16, name="x_grouped", align_bytes=64)
            nc.scalar.copy(out=t[:].bitcast(F32).rearrange("p (b u) -> p b u", u=2),
                           in_=bank_xs[:, 0:2 * P].rearrange("p (u b) -> p b u", u=2))
            x_grouped[i] = t

        def copy_h(i):
            t = work.tile([P, 8 * P], BF16, name="h_grouped", align_bytes=64)
            nc.scalar.copy(out=t[:].bitcast(F32).rearrange("p (g b u) -> p g b u", g=2, u=2),
                           in_=bank_h[:].rearrange("p (g u b) -> p g b u", g=2, u=2))
            h_grouped[i] = t

        def quantize_x(i):
            q = work.tile([P, P], U32, name="x_codes", align_bytes=64)
            s = work.tile([P, P], U8, name="x_scales", align_bytes=64)
            nc.vector.quantize_mx(out=q[:].bitcast(E5M2X4), scales=s[:], in_=x_grouped[i][:])
            codes[(i, 0)], scales[(i, 0)] = q[:], s[:]

        def quantize_h(i):
            q = work.tile([P, 2 * P], U32, name="h_codes", align_bytes=64)
            s = work.tile([P, 2 * P], U8, name="h_scales", align_bytes=64)
            nc.vector.quantize_mx(out=q[:].bitcast(E5M2X4), scales=s[:], in_=h_grouped[i][:])
            for g in range(2):
                codes[(i, 1 + g)], scales[(i, 1 + g)] = q[:, P * g:P * (g + 1)], s[:, P * g:P * (g + 1)]

        def plain_products_and_transposes(i):
            for c in range(2):
                for a in range(2):
                    nc.tensor.matmul(bank_plain[i % 2][c][:], lhsT=st_t[i][:, P * a:P * (a + 1)], rhs=w_t[(a, c)][:],
                                     start=(a == 0), stop=(a == 1))
                    if c == 0:
                        if i + 1 < TILES:
                            transpose_st(i + 1, a)
                        transpose_x(i, a)
                    else:
                        transpose_h(i, a, 0)
                        transpose_h(i, a, 1)

        def add_bias(i, c):
            t = work.tile([P, HALF], F32, name="plain", bufs=5)
            nc.vector.tensor_tensor(out=t[:], in0=bank_plain[i % 2][c][:], in1=bias[c][:], op=ADD)
            plain[(i, c)] = t

        def mx_products(i, col, width, bank):
            c, lo = divmod(col, HALF)
            for g in range(PASSES):
                nc.tensor.matmul_mx(out=bank[:, 0:width], lhsT=codes[(i, g)].bitcast(E5M2X4), lhsT_scale=scales[(i, g)],
                                    rhs=w_codes[(g, c)][:, 2 * lo:2 * (lo + width)].bitcast(E2M1X4),
                                    rhs_scale=w_scales[g][:, col:col + width],
                                    start=(g == 0), stop=(g == PASSES - 1))

        def add_mx(i, col, width, bank):
            c, lo = divmod(col, HALF)
            t = work.tile([P, width], F32, name="summed", bufs=4)
            nc.vector.tensor_tensor(out=t[:], in0=bank[:, 0:width], in1=plain[(i, c)][:, lo:lo + width], op=ADD)
            summed[(i, col)] = t

        def finish(i, col, width):
            t = work.tile([P, width], F32, name="result", bufs=8)
            nc.scalar.activation(out=t[:], in_=summed[(i, col)][:], func=SIGMOID)
            nc.sync.dma_start(out=out_rows[:, i, col:col + width], in_=t[:])

        transpose_st(0, 0)
        transpose_st(0, 1)
        copy_st(0, nc.vector.tensor_copy)
        copy_of_half = (nc.scalar.copy, nc.vector.tensor_copy)
        for c in range(2):
            nc.tensor.matmul(bank_plain[0][c][:], lhsT=ones[:], rhs=bias_rows[:, HALF * c:HALF * (c + 1)],
                             start=True, stop=True)
            copy_of_half[c](out=bias[c][:], in_=bank_plain[0][c][:])
        for a in range(2):
            for c in range(2):
                bank = (bank_mx, bank_plain[1])[a][c][:, 0:2 * P].bitcast(BF16)
                for j in range(4):
                    nc.tensor.transpose(bank[:, P * j:P * (j + 1)], w_raw[a][:, c, S * j:S * (j + 1)], ident_bf[:])
                t = keep.tile([P, HALF], BF16, name="w_t%d%d" % (a, c))
                copy_of_half[c](out=t[:].rearrange("k (p j) -> k p j", j=4),
                                in_=bank.rearrange("k (j p) -> k p j", j=4))
                w_t[(a, c)] = t
        sort_words(0)
        sort_words(1)

        plain_products_and_transposes(0)
        copy_x(0)
        copy_st(1, nc.scalar.copy)
        copy_h(0)
        add_bias(0, 0)
        add_bias(0, 1)
        quantize_x(0)
        quantize_h(0)

        last = TILES - 1
        for i in range(last):
            if i + 2 < TILES:
                sort_words(i + 2)
            plain_products_and_transposes(i + 1)
            copy_x(i + 1)
            if i + 2 < TILES:
                copy_st(i + 2, nc.scalar.copy)
            if i > 0:
                finish(i - 1, HALF, HALF)
            copy_h(i + 1)
            add_bias(i + 1, 0)
            add_bias(i + 1, 1)
            quantize_x(i + 1)
            if i + 1 == last:
                quantize_h(last)
            mx_products(i, 0, HALF, bank_mx[0])
            add_mx(i, 0, HALF, bank_mx[0])
            if i + 1 < last:
                quantize_h(i + 1)
            finish(i, 0, HALF)
            mx_products(i, HALF, HALF, bank_mx[1])
            add_mx(i, HALF, HALF, bank_mx[1])

        finish(last - 1, HALF, HALF)
        quarter = HALF // 2
        pieces = [(0, HALF, bank_plain[0][0]), (HALF, quarter, bank_plain[0][1]), (HALF + quarter, quarter, bank_h)]
        for col, width, bank in pieces:
            mx_products(last, col, width, bank)
            add_mx(last, col, width, bank)
            finish(last, col, width)
